import numpy as np
import ml_dtypes


def mxq(x, axis, fmt="e4m3"):
    dtype, down = {"e4m3": (ml_dtypes.float8_e4m3fn, 7), "e5m2": (ml_dtypes.float8_e5m2, 14)}[fmt]
    v = np.moveaxis(np.asarray(x, np.float32).astype(ml_dtypes.bfloat16).astype(np.float64), axis, -1)
    blocks = v.reshape(v.shape[:-1] + (-1, 32))
    amax = np.abs(blocks).max(-1, keepdims=True)
    byte = np.maximum(np.where(amax > 0, np.frexp(amax)[1] - 1 + 127, 0) - down, 1)
    scale = np.exp2(byte - 127.0)
    codes = (blocks / scale).astype(np.float32).astype(dtype).astype(np.float64)
    return np.moveaxis((codes * scale).reshape(v.shape), -1, axis)


WIDE = False


def mx_kscale(k):
    if not WIDE:
        return np.ones(k)
    levels = np.array([10, -10, 5, -5, 0])
    a = np.random.permutation(np.resize(levels, k // 512 * 4)).reshape(k // 512, 4)
    idx = np.arange(k)
    return np.exp2(a[idx // 512, idx % 128 // 32])


BF16 = ml_dtypes.bfloat16


def bf(x):
    return np.asarray(x, np.float32).astype(BF16)


def f64(x):
    return np.asarray(x).astype(np.float64)


B, N, DIN, H, EMB, CHEB = 8, 512, 448, 64, 10, 3
C = DIN + H
KC = CHEB * C
G = 2 * H


def sigmoid(v):
    return 1.0 / (1.0 + np.exp(-v))


def draw_supports():
    emb = f64(bf(np.random.standard_normal((N, EMB))))
    l = np.maximum((emb[:, None, :] * emb[None, :, :]).sum(-1), 0.0)
    e = np.exp(l - l.max(1, keepdims=True))
    return e / e.sum(1, keepdims=True)


def setup_inputs():
    s = mx_kscale(KC)
    return {"xg": bf(np.random.standard_normal((B, N, KC)) * 0.8 * s),
            "W_gate": bf(np.random.standard_normal((KC, G)) * np.sqrt(2.0 / (KC + G)) / s[:, None]),
            "b_gate": bf(np.random.standard_normal(G) * 0.3),
            "x": bf(np.random.standard_normal((B, N, DIN))),
            "state": bf(np.random.standard_normal((B, N, H))),
            "supports": bf(draw_supports())}


def reference(xg, W_gate, b_gate, x, state, supports):
    z_r = sigmoid((mxq(f64(xg), 2, "e4m3") @ mxq(f64(W_gate), 0, "e4m3")) + f64(b_gate))
    z, r = z_r[..., :H], z_r[..., H:]
    cand = np.concatenate([f64(x), z * f64(state)], -1)
    c1 = mxq(f64(supports), 1, "e4m3") @ mxq(cand, 1, "e4m3")
    return r, cand, c1

@@ -1,0 +1,216 @@
+from contextlib import ExitStack
+
+import concourse.mybir as mybir
+from concourse.masks import make_identity
+
+BF16 = mybir.dt.bfloat16
+F32 = mybir.dt.float32
+U32 = mybir.dt.uint32
+U8 = mybir.dt.uint8
+FP8X4 = mybir.dt.float8_e4m3fn_x4
+
+P = 128
+PACK = 4
+K_PASS = P * PACK
+
+BATCH, NODES, DIN, HID = 8, 512, 448, 64
+FEAT = DIN + HID
+KC = 3 * FEAT
+GATES = 2 * HID
+GATE_PASSES = KC // K_PASS
+ROWS = NODES // P
+
+PREFETCH = 5
+
+FLOPS = 2 * BATCH * NODES * KC * GATES + 2 * BATCH * NODES * NODES * FEAT
+
+
+def words_onto_partitions(nc, banks, identity, blocks, grouped_words):
+    bank = banks.tile([P, 2, 2, P], F32)
+    for s in range(2):
+        for u in range(2):
+            nc.tensor.transpose(out=bank[:, s, u, :], in_=blocks[s][u], identity=identity)
+    nc.scalar.copy(out=grouped_words, in_=bank[:].rearrange("q s u r -> q s r u"))
+
+
+def tile_agcrncell_pb_t_kernel(
+    tc, xg, W_gate, b_gate, x, state, supports, out_0, out_1, out_2
+):
+    nc = tc.nc
+    r_out, cand_out, c1_out = out_0, out_1, out_2
+
+    with ExitStack() as ctx:
+        keep = ctx.enter_context(tc.tile_pool(name="keep", bufs=1))
+        inputs = ctx.enter_context(tc.tile_pool(name="inputs", bufs=PREFETCH + 1))
+        work = ctx.enter_context(tc.tile_pool(name="work", bufs=2))
+        results = ctx.enter_context(tc.tile_pool(name="results", bufs=3))
+        banks = ctx.enter_context(tc.psum_pool(name="banks", bufs=4))
+        gate_banks = ctx.enter_context(tc.psum_pool(name="gate_banks", bufs=1))
+        hop_banks = ctx.enter_context(tc.psum_pool(name="hop_banks", bufs=3))
+
+        xg_tiles = {}
+        x_tiles = {}
+
+        def load(b):
+            xg_tiles[b] = inputs.tile([P, ROWS * KC], BF16, name="xg_sb")
+            nc.sync.dma_start(
+                out=xg_tiles[b][:], in_=xg[b].rearrange("(p j) k -> p (j k)", j=ROWS)
+            )
+            x_tiles[b] = inputs.tile([P, ROWS, DIN], BF16, name="x_sb")
+            nc.sync.dma_start(out=x_tiles[b][:], in_=x[b].rearrange("(p j) f -> p j f", j=ROWS))
+
+        identity = keep.tile([P, P], F32)
+        make_identity(nc, identity[:])
+
+        load(0)
+
+        w_raw = keep.tile([P, GATE_PASSES, PACK, GATES], BF16)
+        nc.sync.dma_start(
+            out=w_raw[:].rearrange("q g (u e) c -> q (g u) (e c)", u=2),
+            in_=W_gate.rearrange("(s q e) c -> q s (e c)", q=P, e=2),
+        )
+        bias = keep.tile([P, GATES], BF16)
+        nc.sync.dma_start(out=bias[:], in_=b_gate.partition_broadcast(P))
+        state_sb = keep.tile([P, BATCH, ROWS, HID], BF16)
+        nc.sync.dma_start(
+            out=state_sb[:].rearrange("p b j h -> p b (j h)"),
+            in_=state.rearrange("b (p j) h -> p b (j h)", j=ROWS),
+        )
+        s_raw = keep.tile([P, ROWS * NODES], BF16)
+        nc.sync.dma_start(out=s_raw[:], in_=supports.rearrange("(p i) m -> p (i m)", i=ROWS))
+
+        for b in range(1, PREFETCH):
+            load(b)
+
+        w_grouped = keep.tile([P, GATE_PASSES, GATES, PACK], BF16, align_bytes=64)
+        nc.vector.tensor_copy(out=w_grouped[:], in_=w_raw[:].rearrange("q g t c -> q g c t"))
+        w_codes = keep.tile([P, GATE_PASSES, GATES], U32, align_bytes=64)
+        w_scales = keep.tile([P, GATE_PASSES, GATES], U8, align_bytes=64)
+        for g in range(GATE_PASSES):
+            nc.vector.quantize_mx(
+                out=w_codes[:, g, :].bitcast(FP8X4),
+                scales=w_scales[:, g, :],
+                in_=w_grouped[:, g, :, :].rearrange("q c t -> q (c t)"),
+            )
+
+        s_words = s_raw[:].bitcast(F32).rearrange("p (i q u) -> p i u q", i=ROWS, u=2)
+        s_grouped = keep.tile([P, ROWS * P * PACK], BF16, align_bytes=64)
+        s_grouped_words = s_grouped[:].bitcast(F32).rearrange("q (i r u) -> q i r u", i=ROWS, u=2)
+        for i in range(0, ROWS, 2):
+            words_onto_partitions(
+                nc,
+                banks,
+                identity[:],
+                [[s_words[:, i + s, u, :] for u in range(2)] for s in range(2)],
+                s_grouped_words[:, i : i + 2, :, :],
+            )
+        s_codes = keep.tile([P, ROWS, P], U32, align_bytes=64)
+        s_scales = keep.tile([P, ROWS, P], U8, align_bytes=64)
+        nc.vector.quantize_mx(
+            out=s_codes[:].rearrange("q i r -> q (i r)").bitcast(FP8X4),
+            scales=s_scales[:].rearrange("q i r -> q (i r)"),
+            in_=s_grouped[:],
+        )
+
+        for b in range(BATCH):
+            if b + PREFETCH < BATCH:
+                load(b + PREFETCH)
+
+            xg_words = xg_tiles[b][:].bitcast(F32).rearrange(
+                "p (j g u q) -> p j g u q", j=ROWS, g=GATE_PASSES, u=2
+            )
+            xg_codes = work.tile([P, GATE_PASSES, ROWS * P], U32, align_bytes=64)
+            xg_scales = work.tile([P, GATE_PASSES, ROWS * P], U8, align_bytes=64)
+            for g in range(GATE_PASSES):
+                xg_grouped = work.tile([P, ROWS * P * PACK], BF16, align_bytes=64)
+                xg_grouped_words = xg_grouped[:].bitcast(F32).rearrange(
+                    "q (j r u) -> q j r u", j=ROWS, u=2
+                )
+                for j in range(0, ROWS, 2):
+                    words_onto_partitions(
+                        nc,
+                        banks,
+                        identity[:],
+                        [[xg_words[:, j + s, g, u, :] for u in range(2)] for s in range(2)],
+                        xg_grouped_words[:, j : j + 2, :, :],
+                    )
+                nc.vector.quantize_mx(
+                    out=xg_codes[:, g, :].bitcast(FP8X4),
+                    scales=xg_scales[:, g, :],
+                    in_=xg_grouped[:],
+                )
+
+            cand_f32 = results.tile([P, ROWS, FEAT], F32)
+            nc.vector.tensor_copy(out=cand_f32[:, :, :DIN], in_=x_tiles[b][:])
+            cand_grouped = work.tile([P, FEAT, PACK], BF16, align_bytes=64)
+            nc.vector.tensor_copy(
+                out=cand_grouped[:, :DIN, :].rearrange("q (c i) t -> q c t i", i=4),
+                in_=x_tiles[b][:].rearrange("q t (c i) -> q c t i", i=4),
+            )
+
+            zr_ps = gate_banks.tile([P, ROWS, GATES], F32)
+            for j in range(ROWS):
+                rows = slice(j * P, (j + 1) * P)
+                for g in range(GATE_PASSES):
+                    nc.tensor.matmul_mx(
+                        out=zr_ps[:, j, :],
+                        lhsT=xg_codes[:, g, rows].bitcast(FP8X4),
+                        lhsT_scale=xg_scales[:, g, rows],
+                        rhs=w_codes[:, g, :].bitcast(FP8X4),
+                        rhs_scale=w_scales[:, g, :],
+                        start=(g == 0),
+                        stop=(g == GATE_PASSES - 1),
+                    )
+            zr_sb = results.tile([P, 2, ROWS, HID], F32)
+            nc.vector.tensor_tensor(
+                out=zr_sb[:].rearrange("p h j c -> p j h c"),
+                in0=zr_ps[:].rearrange("p j (h c) -> p j h c", h=2),
+                in1=bias[:].rearrange("p (o h c) -> p o h c", o=1, h=2).to_broadcast(
+                    [P, ROWS, 2, HID]
+                ),
+                op=mybir.AluOpType.add,
+            )
+            nc.scalar.activation(
+                out=zr_sb[:], in_=zr_sb[:], func=mybir.ActivationFunctionType.Sigmoid
+            )
+            nc.sync.dma_start(
+                out=r_out[b].rearrange("(p j) h -> p j h", j=ROWS), in_=zr_sb[:, 1, :, :]
+            )
+
+            nc.vector.tensor_tensor(
+                out=cand_f32[:, :, DIN:],
+                in0=zr_sb[:, 0, :, :],
+                in1=state_sb[:, b, :, :],
+                op=mybir.AluOpType.mult,
+            )
+            nc.sync.dma_start(
+                out=cand_out[b].rearrange("(p j) f -> p j f", j=ROWS), in_=cand_f32[:]
+            )
+            nc.vector.tensor_copy(
+                out=cand_grouped[:, DIN:, :],
+                in_=cand_f32[:, :, DIN:].rearrange("q t f -> q f t"),
+            )
+            cand_codes = work.tile([P, FEAT], U32, align_bytes=64)
+            cand_scales = work.tile([P, FEAT], U8, align_bytes=64)
+            nc.vector.quantize_mx(
+                out=cand_codes[:].bitcast(FP8X4),
+                scales=cand_scales[:],
+                in_=cand_grouped[:].rearrange("q f t -> q (f t)"),
+            )
+
+            c1_sb = results.tile([P, ROWS, FEAT], F32)
+            for i in range(ROWS):
+                c1_ps = hop_banks.tile([P, FEAT], F32)
+                nc.tensor.matmul_mx(
+                    out=c1_ps[:],
+                    lhsT=s_codes[:, i, :].bitcast(FP8X4),
+                    lhsT_scale=s_scales[:, i, :],
+                    rhs=cand_codes[:].bitcast(FP8X4),
+                    rhs_scale=cand_scales[:],
+                    start=True,
+                    stop=True,
+                )
+                nc.scalar.copy(out=c1_sb[:, i, :], in_=c1_ps[:])
+            nc.sync.dma_start(
+                out=c1_out[b].rearrange("(p i) f -> p i f", i=ROWS), in_=c1_sb[:]
+            )

@@ -47,23 +47,137 @@ def tile_agcrncell_pb_t_kernel(
         banks = ctx.enter_context(tc.psum_pool(name="banks", bufs=4))
         gate_banks = ctx.enter_context(tc.psum_pool(name="gate_banks", bufs=1))
         hop_banks = ctx.enter_context(tc.psum_pool(name="hop_banks", bufs=3))
+        ctx.enter_context(tc.manual_schedule())
 
-        xg_tiles = {}
-        x_tiles = {}
+        xg_sb, x_sb = {}, {}
+        xg_codes, xg_scales = {}, {}
+        zr_sb, cand_f32, cand_grouped = {}, {}, {}
 
         def load(b):
-            xg_tiles[b] = inputs.tile([P, ROWS * KC], BF16, name="xg_sb")
-            nc.sync.dma_start(
-                out=xg_tiles[b][:], in_=xg[b].rearrange("(p j) k -> p (j k)", j=ROWS)
+            xg_sb[b] = inputs.tile([P, ROWS * KC], BF16, name="xg_sb")
+            nc.sync.dma_start(out=xg_sb[b][:], in_=xg[b].rearrange("(p j) k -> p (j k)", j=ROWS))
+            x_sb[b] = inputs.tile([P, ROWS, DIN], BF16, name="x_sb", bufs=PREFETCH + 2)
+            nc.sync.dma_start(out=x_sb[b][:], in_=x[b].rearrange("(p j) f -> p j f", j=ROWS))
+
+        def turn_xg(b):
+            xg_words = xg_sb[b][:].bitcast(F32).rearrange(
+                "p (j g u q) -> p j g u q", j=ROWS, g=GATE_PASSES, u=2
             )
-            x_tiles[b] = inputs.tile([P, ROWS, DIN], BF16, name="x_sb")
-            nc.sync.dma_start(out=x_tiles[b][:], in_=x[b].rearrange("(p j) f -> p j f", j=ROWS))
+            xg_codes[b] = work.tile(
+                [P, GATE_PASSES, ROWS * P], U32, align_bytes=64, name="xg_codes"
+            )
+            xg_scales[b] = work.tile(
+                [P, GATE_PASSES, ROWS * P], U8, align_bytes=64, name="xg_scales"
+            )
+            for g in range(GATE_PASSES):
+                xg_grouped = work.tile(
+                    [P, ROWS * P * PACK], BF16, align_bytes=64, bufs=GATE_PASSES
+                )
+                xg_grouped_words = xg_grouped[:].bitcast(F32).rearrange(
+                    "q (j r u) -> q j r u", j=ROWS, u=2
+                )
+                for j in range(0, ROWS, 2):
+                    words_onto_partitions(
+                        nc,
+                        banks,
+                        identity[:],
+                        [[xg_words[:, j + s, g, u, :] for u in range(2)] for s in range(2)],
+                        xg_grouped_words[:, j : j + 2, :, :],
+                    )
+                nc.vector.quantize_mx(
+                    out=xg_codes[b][:, g, :].bitcast(FP8X4),
+                    scales=xg_scales[b][:, g, :],
+                    in_=xg_grouped[:],
+                )
+
+        def gate_matmul(b):
+            zr_ps = gate_banks.tile([P, ROWS, GATES], F32)
+            for j in range(ROWS):
+                rows = slice(j * P, (j + 1) * P)
+                for g in range(GATE_PASSES):
+                    nc.tensor.matmul_mx(
+                        out=zr_ps[:, j, :],
+                        lhsT=xg_codes[b][:, g, rows].bitcast(FP8X4),
+                        lhsT_scale=xg_scales[b][:, g, rows],
+                        rhs=w_codes[:, g, :].bitcast(FP8X4),
+                        rhs_scale=w_scales[:, g, :],
+                        start=(g == 0),
+                        stop=(g == GATE_PASSES - 1),
+                    )
+            zr_sb[b] = results.tile([P, 2, ROWS, HID], F32, name="zr_sb")
+            nc.vector.tensor_tensor(
+                out=zr_sb[b][:].rearrange("p h j c -> p j h c"),
+                in0=zr_ps[:].rearrange("p j (h c) -> p j h c", h=2),
+                in1=bias[:].rearrange("p (o h c) -> p o h c", o=1, h=2).to_broadcast(
+                    [P, ROWS, 2, HID]
+                ),
+                op=mybir.AluOpType.add,
+            )
+
+        def x_part(b):
+            cand_f32[b] = results.tile([P, ROWS, FEAT], F32, name="cand_f32")
+            nc.vector.tensor_copy(out=cand_f32[b][:, :, :DIN], in_=x_sb[b][:])
+            cand_grouped[b] = work.tile(
+                [P, FEAT, PACK], BF16, align_bytes=64, name="cand_grouped"
+            )
+            nc.vector.tensor_copy(
+                out=cand_grouped[b][:, :DIN, :].rearrange("q (c i) t -> q c t i", i=4),
+                in_=x_sb[b][:].rearrange("q t (c i) -> q c t i", i=4),
+            )
+
+        def gate_sigmoid(b):
+            nc.scalar.activation(
+                out=zr_sb[b][:], in_=zr_sb[b][:], func=mybir.ActivationFunctionType.Sigmoid
+            )
+            nc.sync.dma_start(
+                out=r_out[b].rearrange("(p j) h -> p j h", j=ROWS), in_=zr_sb[b][:, 1, :, :]
+            )
+
+        def finish_cand(b):
+            nc.vector.tensor_tensor(
+                out=cand_f32[b][:, :, DIN:],
+                in0=zr_sb[b][:, 0, :, :],
+                in1=state_sb[:, b, :, :],
+                op=mybir.AluOpType.mult,
+            )
+            nc.sync.dma_start(
+                out=cand_out[b].rearrange("(p j) f -> p j f", j=ROWS), in_=cand_f32[b][:]
+            )
+            nc.vector.tensor_copy(
+                out=cand_grouped[b][:, DIN:, :],
+                in_=cand_f32[b][:, :, DIN:].rearrange("q t f -> q f t"),
+            )
+            cand_codes = work.tile([P, FEAT], U32, align_bytes=64)
+            cand_scales = work.tile([P, FEAT], U8, align_bytes=64)
+            nc.vector.quantize_mx(
+                out=cand_codes[:].bitcast(FP8X4),
+                scales=cand_scales[:],
+                in_=cand_grouped[b][:].rearrange("q f t -> q (f t)"),
+            )
+            return cand_codes, cand_scales
+
+        def hop(b, cand_codes, cand_scales):
+            c1_sb = results.tile([P, ROWS, FEAT], F32)
+            for i in range(ROWS):
+                c1_ps = hop_banks.tile([P, FEAT], F32)
+                nc.tensor.matmul_mx(
+                    out=c1_ps[:],
+                    lhsT=s_codes[:, i, :].bitcast(FP8X4),
+                    lhsT_scale=s_scales[:, i, :],
+                    rhs=cand_codes[:].bitcast(FP8X4),
+                    rhs_scale=cand_scales[:],
+                    start=True,
+                    stop=True,
+                )
+                nc.scalar.copy(out=c1_sb[:, i, :], in_=c1_ps[:])
+            nc.sync.dma_start(out=c1_out[b].rearrange("(p i) f -> p i f", i=ROWS), in_=c1_sb[:])
 
         identity = keep.tile([P, P], F32)
         make_identity(nc, identity[:])
 
+        s_raw = keep.tile([P, ROWS * NODES], BF16)
+        nc.sync.dma_start(out=s_raw[:], in_=supports.rearrange("(p i) m -> p (i m)", i=ROWS))
         load(0)
-
         w_raw = keep.tile([P, GATE_PASSES, PACK, GATES], BF16)
         nc.sync.dma_start(
             out=w_raw[:].rearrange("q g (u e) c -> q (g u) (e c)", u=2),
@@ -71,27 +185,14 @@ def tile_agcrncell_pb_t_kernel(
         )
         bias = keep.tile([P, GATES], BF16)
         nc.sync.dma_start(out=bias[:], in_=b_gate.partition_broadcast(P))
+        load(1)
         state_sb = keep.tile([P, BATCH, ROWS, HID], BF16)
         nc.sync.dma_start(
             out=state_sb[:].rearrange("p b j h -> p b (j h)"),
             in_=state.rearrange("b (p j) h -> p b (j h)", j=ROWS),
         )
-        s_raw = keep.tile([P, ROWS * NODES], BF16)
-        nc.sync.dma_start(out=s_raw[:], in_=supports.rearrange("(p i) m -> p (i m)", i=ROWS))
-
-        for b in range(1, PREFETCH):
+        for b in range(2, PREFETCH):
             load(b)
-
-        w_grouped = keep.tile([P, GATE_PASSES, GATES, PACK], BF16, align_bytes=64)
-        nc.vector.tensor_copy(out=w_grouped[:], in_=w_raw[:].rearrange("q g t c -> q g c t"))
-        w_codes = keep.tile([P, GATE_PASSES, GATES], U32, align_bytes=64)
-        w_scales = keep.tile([P, GATE_PASSES, GATES], U8, align_bytes=64)
-        for g in range(GATE_PASSES):
-            nc.vector.quantize_mx(
-                out=w_codes[:, g, :].bitcast(FP8X4),
-                scales=w_scales[:, g, :],
-                in_=w_grouped[:, g, :, :].rearrange("q c t -> q (c t)"),
-            )
 
         s_words = s_raw[:].bitcast(F32).rearrange("p (i q u) -> p i u q", i=ROWS, u=2)
         s_grouped = keep.tile([P, ROWS * P * PACK], BF16, align_bytes=64)
@@ -112,105 +213,29 @@ def tile_agcrncell_pb_t_kernel(
             in_=s_grouped[:],
         )
 
-        for b in range(BATCH):
-            if b + PREFETCH < BATCH:
-                load(b + PREFETCH)
-
-            xg_words = xg_tiles[b][:].bitcast(F32).rearrange(
-                "p (j g u q) -> p j g u q", j=ROWS, g=GATE_PASSES, u=2
-            )
-            xg_codes = work.tile([P, GATE_PASSES, ROWS * P], U32, align_bytes=64)
-            xg_scales = work.tile([P, GATE_PASSES, ROWS * P], U8, align_bytes=64)
-            for g in range(GATE_PASSES):
-                xg_grouped = work.tile([P, ROWS * P * PACK], BF16, align_bytes=64)
-                xg_grouped_words = xg_grouped[:].bitcast(F32).rearrange(
-                    "q (j r u) -> q j r u", j=ROWS, u=2
-                )
-                for j in range(0, ROWS, 2):
-                    words_onto_partitions(
-                        nc,
-                        banks,
-                        identity[:],
-                        [[xg_words[:, j + s, g, u, :] for u in range(2)] for s in range(2)],
-                        xg_grouped_words[:, j : j + 2, :, :],
-                    )
-                nc.vector.quantize_mx(
-                    out=xg_codes[:, g, :].bitcast(FP8X4),
-                    scales=xg_scales[:, g, :],
-                    in_=xg_grouped[:],
-                )
-
-            cand_f32 = results.tile([P, ROWS, FEAT], F32)
-            nc.vector.tensor_copy(out=cand_f32[:, :, :DIN], in_=x_tiles[b][:])
-            cand_grouped = work.tile([P, FEAT, PACK], BF16, align_bytes=64)
-            nc.vector.tensor_copy(
-                out=cand_grouped[:, :DIN, :].rearrange("q (c i) t -> q c t i", i=4),
-                in_=x_tiles[b][:].rearrange("q t (c i) -> q c t i", i=4),
-            )
-
-            zr_ps = gate_banks.tile([P, ROWS, GATES], F32)
-            for j in range(ROWS):
-                rows = slice(j * P, (j + 1) * P)
-                for g in range(GATE_PASSES):
-                    nc.tensor.matmul_mx(
-                        out=zr_ps[:, j, :],
-                        lhsT=xg_codes[:, g, rows].bitcast(FP8X4),
-                        lhsT_scale=xg_scales[:, g, rows],
-                        rhs=w_codes[:, g, :].bitcast(FP8X4),
-                        rhs_scale=w_scales[:, g, :],
-                        start=(g == 0),
-                        stop=(g == GATE_PASSES - 1),
-                    )
-            zr_sb = results.tile([P, 2, ROWS, HID], F32)
-            nc.vector.tensor_tensor(
-                out=zr_sb[:].rearrange("p h j c -> p j h c"),
-                in0=zr_ps[:].rearrange("p j (h c) -> p j h c", h=2),
-                in1=bias[:].rearrange("p (o h c) -> p o h c", o=1, h=2).to_broadcast(
-                    [P, ROWS, 2, HID]
-                ),
-                op=mybir.AluOpType.add,
-            )
-            nc.scalar.activation(
-                out=zr_sb[:], in_=zr_sb[:], func=mybir.ActivationFunctionType.Sigmoid
-            )
-            nc.sync.dma_start(
-                out=r_out[b].rearrange("(p j) h -> p j h", j=ROWS), in_=zr_sb[:, 1, :, :]
-            )
-
-            nc.vector.tensor_tensor(
-                out=cand_f32[:, :, DIN:],
-                in0=zr_sb[:, 0, :, :],
-                in1=state_sb[:, b, :, :],
-                op=mybir.AluOpType.mult,
-            )
-            nc.sync.dma_start(
-                out=cand_out[b].rearrange("(p j) f -> p j f", j=ROWS), in_=cand_f32[:]
-            )
-            nc.vector.tensor_copy(
-                out=cand_grouped[:, DIN:, :],
-                in_=cand_f32[:, :, DIN:].rearrange("q t f -> q f t"),
-            )
-            cand_codes = work.tile([P, FEAT], U32, align_bytes=64)
-            cand_scales = work.tile([P, FEAT], U8, align_bytes=64)
+        w_grouped = keep.tile([P, GATE_PASSES, GATES, PACK], BF16, align_bytes=64)
+        nc.vector.tensor_copy(out=w_grouped[:], in_=w_raw[:].rearrange("q g t c -> q g c t"))
+        w_codes = keep.tile([P, GATE_PASSES, GATES], U32, align_bytes=64)
+        w_scales = keep.tile([P, GATE_PASSES, GATES], U8, align_bytes=64)
+        for g in range(GATE_PASSES):
             nc.vector.quantize_mx(
-                out=cand_codes[:].bitcast(FP8X4),
-                scales=cand_scales[:],
-                in_=cand_grouped[:].rearrange("q f t -> q (f t)"),
+                out=w_codes[:, g, :].bitcast(FP8X4),
+                scales=w_scales[:, g, :],
+                in_=w_grouped[:, g, :, :].rearrange("q c t -> q (c t)"),
             )
 
-            c1_sb = results.tile([P, ROWS, FEAT], F32)
-            for i in range(ROWS):
-                c1_ps = hop_banks.tile([P, FEAT], F32)
-                nc.tensor.matmul_mx(
-                    out=c1_ps[:],
-                    lhsT=s_codes[:, i, :].bitcast(FP8X4),
-                    lhsT_scale=s_scales[:, i, :],
-                    rhs=cand_codes[:].bitcast(FP8X4),
-                    rhs_scale=cand_scales[:],
-                    start=True,
-                    stop=True,
-                )
-                nc.scalar.copy(out=c1_sb[:, i, :], in_=c1_ps[:])
-            nc.sync.dma_start(
-                out=c1_out[b].rearrange("(p i) f -> p i f", i=ROWS), in_=c1_sb[:]
-            )
+        for step in range(BATCH + 2):
+            first, second, third = step, step - 1, step - 2
+            if first + PREFETCH < BATCH:
+                load(first + PREFETCH)
+            if third >= 0:
+                cand_codes, cand_scales = finish_cand(third)
+            if first < BATCH:
+                turn_xg(first)
+            if 0 <= second < BATCH:
+                gate_matmul(second)
+                x_part(second)
+            if third >= 0:
+                hop(third, cand_codes, cand_scales)
+            if 0 <= second < BATCH:
+                gate_sigmoid(second)

@@ -20,7 +20,7 @@ GATES = 2 * HID
 GATE_PASSES = KC // K_PASS
 ROWS = NODES // P
 
-PREFETCH = 5
+PREFETCH = 3
 
 FLOPS = 2 * BATCH * NODES * KC * GATES + 2 * BATCH * NODES * NODES * FEAT
 
@@ -43,7 +43,7 @@ def tile_agcrncell_pb_t_kernel(
         keep = ctx.enter_context(tc.tile_pool(name="keep", bufs=1))
         inputs = ctx.enter_context(tc.tile_pool(name="inputs", bufs=PREFETCH + 1))
         work = ctx.enter_context(tc.tile_pool(name="work", bufs=2))
-        results = ctx.enter_context(tc.tile_pool(name="results", bufs=3))
+        results = ctx.enter_context(tc.tile_pool(name="results", bufs=4))
         banks = ctx.enter_context(tc.psum_pool(name="banks", bufs=4))
         gate_banks = ctx.enter_context(tc.psum_pool(name="gate_banks", bufs=1))
         hop_banks = ctx.enter_context(tc.psum_pool(name="hop_banks", bufs=3))
@@ -54,40 +54,48 @@ def tile_agcrncell_pb_t_kernel(
         zr_sb, cand_f32, cand_grouped = {}, {}, {}
 
         def load(b):
-            xg_sb[b] = inputs.tile([P, ROWS * KC], BF16, name="xg_sb")
-            nc.sync.dma_start(out=xg_sb[b][:], in_=xg[b].rearrange("(p j) k -> p (j k)", j=ROWS))
+            xg_halves = xg[b].rearrange("(p h j) k -> p h (j k)", h=2, j=ROWS // 2)
+            xg_sb[b] = []
+            for half in range(2):
+                xg_half = inputs.tile([P, ROWS // 2 * KC], BF16, bufs=2 * (PREFETCH + 1))
+                nc.sync.dma_start(out=xg_half[:], in_=xg_halves[:, half, :])
+                xg_sb[b].append(xg_half)
             x_sb[b] = inputs.tile([P, ROWS, DIN], BF16, name="x_sb", bufs=PREFETCH + 2)
             nc.sync.dma_start(out=x_sb[b][:], in_=x[b].rearrange("(p j) f -> p j f", j=ROWS))
 
         def turn_xg(b):
-            xg_words = xg_sb[b][:].bitcast(F32).rearrange(
-                "p (j g u q) -> p j g u q", j=ROWS, g=GATE_PASSES, u=2
-            )
             xg_codes[b] = work.tile(
                 [P, GATE_PASSES, ROWS * P], U32, align_bytes=64, name="xg_codes"
             )
             xg_scales[b] = work.tile(
                 [P, GATE_PASSES, ROWS * P], U8, align_bytes=64, name="xg_scales"
             )
-            for g in range(GATE_PASSES):
-                xg_grouped = work.tile(
-                    [P, ROWS * P * PACK], BF16, align_bytes=64, bufs=GATE_PASSES
+            xg_grouped = [
+                work.tile(
+                    [P, ROWS * P * PACK], BF16, align_bytes=64, name="xg_grouped", bufs=GATE_PASSES
                 )
-                xg_grouped_words = xg_grouped[:].bitcast(F32).rearrange(
-                    "q (j r u) -> q j r u", j=ROWS, u=2
+                for g in range(GATE_PASSES)
+            ]
+            for half in range(2):
+                xg_words = xg_sb[b][half][:].bitcast(F32).rearrange(
+                    "p (s g u q) -> p s g u q", s=2, g=GATE_PASSES, u=2
                 )
-                for j in range(0, ROWS, 2):
+                for g in range(GATE_PASSES):
+                    xg_grouped_words = xg_grouped[g][:].bitcast(F32).rearrange(
+                        "q (j r u) -> q j r u", j=ROWS, u=2
+                    )
                     words_onto_partitions(
                         nc,
                         banks,
                         identity[:],
-                        [[xg_words[:, j + s, g, u, :] for u in range(2)] for s in range(2)],
-                        xg_grouped_words[:, j : j + 2, :, :],
+                        [[xg_words[:, s, g, u, :] for u in range(2)] for s in range(2)],
+                        xg_grouped_words[:, 2 * half : 2 * half + 2, :, :],
                     )
+            for g in range(GATE_PASSES):
                 nc.vector.quantize_mx(
                     out=xg_codes[b][:, g, :].bitcast(FP8X4),
                     scales=xg_scales[b][:, g, :],
-                    in_=xg_grouped[:],
+                    in_=xg_grouped[g][:],
                 )
 
         def gate_matmul(b):
@@ -158,6 +166,8 @@ def tile_agcrncell_pb_t_kernel(
 
         def hop(b, cand_codes, cand_scales):
             c1_sb = results.tile([P, ROWS, FEAT], F32)
+            c1_rows = c1_out[b].rearrange("(p i) f -> p i f", i=ROWS)
+            rows_a_store = 1 if b == BATCH - 1 else ROWS
             for i in range(ROWS):
                 c1_ps = hop_banks.tile([P, FEAT], F32)
                 nc.tensor.matmul_mx(
@@ -170,13 +180,13 @@ def tile_agcrncell_pb_t_kernel(
                     stop=True,
                 )
                 nc.scalar.copy(out=c1_sb[:, i, :], in_=c1_ps[:])
-            nc.sync.dma_start(out=c1_out[b].rearrange("(p i) f -> p i f", i=ROWS), in_=c1_sb[:])
+                if (i + 1) % rows_a_store == 0:
+                    ready = slice(i + 1 - rows_a_store, i + 1)
+                    nc.sync.dma_start(out=c1_rows[:, ready, :], in_=c1_sb[:, ready, :])
 
         identity = keep.tile([P, P], F32)
         make_identity(nc, identity[:])
 
-        s_raw = keep.tile([P, ROWS * NODES], BF16)
-        nc.sync.dma_start(out=s_raw[:], in_=supports.rearrange("(p i) m -> p (i m)", i=ROWS))
         load(0)
         w_raw = keep.tile([P, GATE_PASSES, PACK, GATES], BF16)
         nc.sync.dma_start(
@@ -185,6 +195,8 @@ def tile_agcrncell_pb_t_kernel(
         )
         bias = keep.tile([P, GATES], BF16)
         nc.sync.dma_start(out=bias[:], in_=b_gate.partition_broadcast(P))
+        s_raw = keep.tile([P, ROWS * NODES], BF16)
+        nc.sync.dma_start(out=s_raw[:], in_=supports.rearrange("(p i) m -> p (i m)", i=ROWS))
         load(1)
         state_sb = keep.tile([P, BATCH, ROWS, HID], BF16)
         nc.sync.dma_start(
@@ -194,34 +206,39 @@ def tile_agcrncell_pb_t_kernel(
         for b in range(2, PREFETCH):
             load(b)
 
-        s_words = s_raw[:].bitcast(F32).rearrange("p (i q u) -> p i u q", i=ROWS, u=2)
-        s_grouped = keep.tile([P, ROWS * P * PACK], BF16, align_bytes=64)
-        s_grouped_words = s_grouped[:].bitcast(F32).rearrange("q (i r u) -> q i r u", i=ROWS, u=2)
-        for i in range(0, ROWS, 2):
-            words_onto_partitions(
-                nc,
-                banks,
-                identity[:],
-                [[s_words[:, i + s, u, :] for u in range(2)] for s in range(2)],
-                s_grouped_words[:, i : i + 2, :, :],
-            )
-        s_codes = keep.tile([P, ROWS, P], U32, align_bytes=64)
-        s_scales = keep.tile([P, ROWS, P], U8, align_bytes=64)
-        nc.vector.quantize_mx(
-            out=s_codes[:].rearrange("q i r -> q (i r)").bitcast(FP8X4),
-            scales=s_scales[:].rearrange("q i r -> q (i r)"),
-            in_=s_grouped[:],
-        )
-
-        w_grouped = keep.tile([P, GATE_PASSES, GATES, PACK], BF16, align_bytes=64)
-        nc.vector.tensor_copy(out=w_grouped[:], in_=w_raw[:].rearrange("q g t c -> q g c t"))
         w_codes = keep.tile([P, GATE_PASSES, GATES], U32, align_bytes=64)
         w_scales = keep.tile([P, GATE_PASSES, GATES], U8, align_bytes=64)
-        for g in range(GATE_PASSES):
+        s_codes = keep.tile([P, ROWS, P], U32, align_bytes=64)
+        s_scales = keep.tile([P, ROWS, P], U8, align_bytes=64)
+
+        def quantise_w_gate():
+            w_grouped = keep.tile([P, GATE_PASSES, GATES, PACK], BF16, align_bytes=64)
+            nc.vector.tensor_copy(out=w_grouped[:], in_=w_raw[:].rearrange("q g t c -> q g c t"))
+            for g in range(GATE_PASSES):
+                nc.vector.quantize_mx(
+                    out=w_codes[:, g, :].bitcast(FP8X4),
+                    scales=w_scales[:, g, :],
+                    in_=w_grouped[:, g, :, :].rearrange("q c t -> q (c t)"),
+                )
+
+        def turn_supports():
+            s_words = s_raw[:].bitcast(F32).rearrange("p (i q u) -> p i u q", i=ROWS, u=2)
+            s_grouped = keep.tile([P, ROWS * P * PACK], BF16, align_bytes=64)
+            s_grouped_words = s_grouped[:].bitcast(F32).rearrange(
+                "q (i r u) -> q i r u", i=ROWS, u=2
+            )
+            for i in range(0, ROWS, 2):
+                words_onto_partitions(
+                    nc,
+                    banks,
+                    identity[:],
+                    [[s_words[:, i + s, u, :] for u in range(2)] for s in range(2)],
+                    s_grouped_words[:, i : i + 2, :, :],
+                )
             nc.vector.quantize_mx(
-                out=w_codes[:, g, :].bitcast(FP8X4),
-                scales=w_scales[:, g, :],
-                in_=w_grouped[:, g, :, :].rearrange("q c t -> q (c t)"),
+                out=s_codes[:].rearrange("q i r -> q (i r)").bitcast(FP8X4),
+                scales=s_scales[:].rearrange("q i r -> q (i r)"),
+                in_=s_grouped[:],
             )
 
         for step in range(BATCH + 2):
@@ -232,6 +249,9 @@ def tile_agcrncell_pb_t_kernel(
                 cand_codes, cand_scales = finish_cand(third)
             if first < BATCH:
                 turn_xg(first)
+            if step == 0:
+                quantise_w_gate()
+                turn_supports()
             if 0 <= second < BATCH:
                 gate_matmul(second)
                 x_part(second)

@@ -193,8 +193,11 @@ def tile_agcrncell_pb_t_kernel(
             out=w_raw[:].rearrange("q g (u e) c -> q (g u) (e c)", u=2),
             in_=W_gate.rearrange("(s q e) c -> q s (e c)", q=P, e=2),
         )
-        bias = keep.tile([P, GATES], BF16)
-        nc.sync.dma_start(out=bias[:], in_=b_gate.partition_broadcast(P))
+        bias_rows = keep.tile([P, GATES], BF16)
+        nc.vector.memset(bias_rows[:], 0.0)
+        nc.sync.dma_start(out=bias_rows[0:1, :], in_=b_gate.rearrange("(o c) -> o c", o=1))
+        ones = keep.tile([P, P], BF16)
+        nc.vector.memset(ones[:], 1.0)
         s_raw = keep.tile([P, ROWS * NODES], BF16)
         nc.sync.dma_start(out=s_raw[:], in_=supports.rearrange("(p i) m -> p (i m)", i=ROWS))
         load(1)
@@ -210,6 +213,13 @@ def tile_agcrncell_pb_t_kernel(
         w_scales = keep.tile([P, GATE_PASSES, GATES], U8, align_bytes=64)
         s_codes = keep.tile([P, ROWS, P], U32, align_bytes=64)
         s_scales = keep.tile([P, ROWS, P], U8, align_bytes=64)
+
+        bias = keep.tile([P, GATES], F32)
+
+        def spread_bias():
+            bias_ps = banks.tile([P, GATES], F32, tag="bank")
+            nc.tensor.matmul(out=bias_ps[:], lhsT=ones[:], rhs=bias_rows[:], start=True, stop=True)
+            nc.scalar.copy(out=bias[:], in_=bias_ps[:])
 
         def quantise_w_gate():
             w_grouped = keep.tile([P, GATE_PASSES, GATES, PACK], BF16, align_bytes=64)
@@ -250,6 +260,7 @@ def tile_agcrncell_pb_t_kernel(
             if first < BATCH:
                 turn_xg(first)
             if step == 0:
+                spread_bias()
                 quantise_w_gate()
                 turn_supports()
             if 0 <= second < BATCH:

@@ -54,12 +54,8 @@ def tile_agcrncell_pb_t_kernel(
         zr_sb, cand_f32, cand_grouped = {}, {}, {}
 
         def load(b):
-            xg_halves = xg[b].rearrange("(p h j) k -> p h (j k)", h=2, j=ROWS // 2)
-            xg_sb[b] = []
-            for half in range(2):
-                xg_half = inputs.tile([P, ROWS // 2 * KC], BF16, bufs=2 * (PREFETCH + 1))
-                nc.sync.dma_start(out=xg_half[:], in_=xg_halves[:, half, :])
-                xg_sb[b].append(xg_half)
+            xg_sb[b] = inputs.tile([P, ROWS * KC], BF16, name="xg_sb")
+            nc.sync.dma_start(out=xg_sb[b][:], in_=xg[b].rearrange("(p j) k -> p (j k)", j=ROWS))
             x_sb[b] = inputs.tile([P, ROWS, DIN], BF16, name="x_sb", bufs=PREFETCH + 2)
             nc.sync.dma_start(out=x_sb[b][:], in_=x[b].rearrange("(p j) f -> p j f", j=ROWS))
 
@@ -76,10 +72,10 @@ def tile_agcrncell_pb_t_kernel(
                 )
                 for g in range(GATE_PASSES)
             ]
-            for half in range(2):
-                xg_words = xg_sb[b][half][:].bitcast(F32).rearrange(
-                    "p (s g u q) -> p s g u q", s=2, g=GATE_PASSES, u=2
-                )
+            xg_words = xg_sb[b][:].bitcast(F32).rearrange(
+                "p (j g u q) -> p j g u q", j=ROWS, g=GATE_PASSES, u=2
+            )
+            for j in range(0, ROWS, 2):
                 for g in range(GATE_PASSES):
                     xg_grouped_words = xg_grouped[g][:].bitcast(F32).rearrange(
                         "q (j r u) -> q j r u", j=ROWS, u=2
@@ -88,8 +84,8 @@ def tile_agcrncell_pb_t_kernel(
                         nc,
                         banks,
                         identity[:],
-                        [[xg_words[:, s, g, u, :] for u in range(2)] for s in range(2)],
-                        xg_grouped_words[:, 2 * half : 2 * half + 2, :, :],
+                        [[xg_words[:, j + s, g, u, :] for u in range(2)] for s in range(2)],
+                        xg_grouped_words[:, j : j + 2, :, :],
                     )
             for g in range(GATE_PASSES):
                 nc.vector.quantize_mx(

@@ -183,25 +183,21 @@ def tile_agcrncell_pb_t_kernel(
         identity = keep.tile([P, P], F32)
         make_identity(nc, identity[:])
 
-        load(0)
-        w_raw = keep.tile([P, GATE_PASSES, PACK, GATES], BF16)
+        w_lin = keep.tile([P, KC // P * GATES], BF16)
+        nc.sync.dma_start(out=w_lin[:], in_=W_gate.rearrange("(p i) c -> p (i c)", p=P))
+        st_lin = keep.tile([P, BATCH * NODES // P * HID], BF16)
         nc.sync.dma_start(
-            out=w_raw[:].rearrange("q g (u e) c -> q (g u) (e c)", u=2),
-            in_=W_gate.rearrange("(s q e) c -> q s (e c)", q=P, e=2),
+            out=st_lin[:], in_=state.flatten_outer_dims().rearrange("(p r) h -> p (r h)", p=P)
         )
         bias_rows = keep.tile([P, GATES], BF16)
         nc.vector.memset(bias_rows[:], 0.0)
         nc.sync.dma_start(out=bias_rows[0:1, :], in_=b_gate.rearrange("(o c) -> o c", o=1))
         ones = keep.tile([P, P], BF16)
         nc.vector.memset(ones[:], 1.0)
+        load(0)
         s_raw = keep.tile([P, ROWS * NODES], BF16)
         nc.sync.dma_start(out=s_raw[:], in_=supports.rearrange("(p i) m -> p (i m)", i=ROWS))
         load(1)
-        state_sb = keep.tile([P, BATCH, ROWS, HID], BF16)
-        nc.sync.dma_start(
-            out=state_sb[:].rearrange("p b j h -> p b (j h)"),
-            in_=state.rearrange("b (p j) h -> p b (j h)", j=ROWS),
-        )
         for b in range(2, PREFETCH):
             load(b)
 
@@ -216,6 +212,47 @@ def tile_agcrncell_pb_t_kernel(
             bias_ps = banks.tile([P, GATES], F32, tag="bank")
             nc.tensor.matmul(out=bias_ps[:], lhsT=ones[:], rhs=bias_rows[:], start=True, stop=True)
             nc.scalar.copy(out=bias[:], in_=bias_ps[:])
+
+        def turned(words, count):
+            filled = []
+            for first in range(0, count, 4):
+                bank = banks.tile([P, 4, P], F32, tag="bank", name="turned_bank")
+                for n in range(first, min(first + 4, count)):
+                    nc.tensor.transpose(
+                        out=bank[:, n - first, :], in_=words[:, n * P : (n + 1) * P], identity=identity[:]
+                    )
+                filled.append(bank[:, : min(4, count - first), :])
+            return filled
+
+        w_raw = keep.tile([P, GATE_PASSES, PACK, GATES], BF16)
+
+        def sort_w_gate():
+            pairs_of_rows = KC // P // 2
+            w_half = keep.tile([P, P, pairs_of_rows], F32)
+            low, high = turned(w_lin[:].bitcast(F32), pairs_of_rows)
+            nc.scalar.copy(out=w_half[:, :, :4], in_=low.rearrange("q m p -> q p m"))
+            nc.vector.tensor_copy(out=w_half[:, :, 4:], in_=high.rearrange("q m p -> q p m"))
+            low, high = turned(w_half[:].rearrange("q p m -> q (p m)"), pairs_of_rows)
+            w_raw_words = w_raw[:].rearrange("q g t c -> q (g t c)").bitcast(F32).rearrange(
+                "q (s w) -> q s w", w=P
+            )
+            nc.scalar.copy(out=w_raw_words[:, :4, :], in_=low)
+            nc.vector.tensor_copy(out=w_raw_words[:, 4:, :], in_=high)
+
+        state_sb = keep.tile([P, BATCH, ROWS, HID], BF16)
+
+        def sort_state():
+            blocks = BATCH * NODES // P // ROWS
+            st_half = keep.tile([P, P, blocks], F32)
+            low, high = turned(st_lin[:].bitcast(F32), blocks)
+            nc.scalar.copy(out=st_half[:, :, :4], in_=low.rearrange("q v p -> q p v"))
+            nc.vector.tensor_copy(out=st_half[:, :, 4:], in_=high.rearrange("q v p -> q p v"))
+            low, high = turned(st_half[:].rearrange("q p v -> q (p v)"), BATCH)
+            state_words = state_sb[:].rearrange("p b j h -> p (b j h)").bitcast(F32).rearrange(
+                "p (b w) -> p b w", b=BATCH
+            )
+            nc.scalar.copy(out=state_words[:, :4, :], in_=low)
+            nc.vector.tensor_copy(out=state_words[:, 4:, :], in_=high)
 
         def quantise_w_gate():
             w_grouped = keep.tile([P, GATE_PASSES, GATES, PACK], BF16, align_bytes=64)
@@ -247,6 +284,11 @@ def tile_agcrncell_pb_t_kernel(
                 in_=s_grouped[:],
             )
 
+        sort_w_gate()
+        sort_state()
+        quantise_w_gate()
+        spread_bias()
+
         for step in range(BATCH + 2):
             first, second, third = step, step - 1, step - 2
             if first + PREFETCH < BATCH:
@@ -256,8 +298,6 @@ def tile_agcrncell_pb_t_kernel(
             if first < BATCH:
                 turn_xg(first)
             if step == 0:
-                spread_bias()
-                quantise_w_gate()
                 turn_supports()
             if 0 <= second < BATCH:
                 gate_matmul(second)

@@ -20,6 +20,8 @@ GATES = 2 * HID
 GATE_PASSES = KC // K_PASS
 ROWS = NODES // P
 
+DMA_ALIGN = 256
+
 PREFETCH = 3
 
 FLOPS = 2 * BATCH * NODES * KC * GATES + 2 * BATCH * NODES * NODES * FEAT
@@ -54,9 +56,11 @@ def tile_agcrncell_pb_t_kernel(
         zr_sb, cand_f32, cand_grouped = {}, {}, {}
 
         def load(b):
-            xg_sb[b] = inputs.tile([P, ROWS * KC], BF16, name="xg_sb")
+            xg_sb[b] = inputs.tile([P, ROWS * KC], BF16, align_bytes=DMA_ALIGN, name="xg_sb")
             nc.sync.dma_start(out=xg_sb[b][:], in_=xg[b].rearrange("(p j) k -> p (j k)", j=ROWS))
-            x_sb[b] = inputs.tile([P, ROWS, DIN], BF16, name="x_sb", bufs=PREFETCH + 2)
+            x_sb[b] = inputs.tile(
+                [P, ROWS, DIN], BF16, align_bytes=DMA_ALIGN, name="x_sb", bufs=PREFETCH + 2
+            )
             nc.sync.dma_start(out=x_sb[b][:], in_=x[b].rearrange("(p j) f -> p j f", j=ROWS))
 
         def turn_xg(b):
@@ -108,7 +112,7 @@ def tile_agcrncell_pb_t_kernel(
                         start=(g == 0),
                         stop=(g == GATE_PASSES - 1),
                     )
-            zr_sb[b] = results.tile([P, 2, ROWS, HID], F32, name="zr_sb")
+            zr_sb[b] = results.tile([P, 2, ROWS, HID], F32, align_bytes=DMA_ALIGN, name="zr_sb")
             nc.vector.tensor_tensor(
                 out=zr_sb[b][:].rearrange("p h j c -> p j h c"),
                 in0=zr_ps[:].rearrange("p j (h c) -> p j h c", h=2),
@@ -119,7 +123,7 @@ def tile_agcrncell_pb_t_kernel(
             )
 
         def x_part(b):
-            cand_f32[b] = results.tile([P, ROWS, FEAT], F32, name="cand_f32")
+            cand_f32[b] = results.tile([P, ROWS, FEAT], F32, align_bytes=DMA_ALIGN, name="cand_f32")
             nc.vector.tensor_copy(out=cand_f32[b][:, :, :DIN], in_=x_sb[b][:])
             cand_grouped[b] = work.tile(
                 [P, FEAT, PACK], BF16, align_bytes=64, name="cand_grouped"
@@ -161,7 +165,7 @@ def tile_agcrncell_pb_t_kernel(
             return cand_codes, cand_scales
 
         def hop(b, cand_codes, cand_scales):
-            c1_sb = results.tile([P, ROWS, FEAT], F32)
+            c1_sb = results.tile([P, ROWS, FEAT], F32, align_bytes=DMA_ALIGN)
             c1_rows = c1_out[b].rearrange("(p i) f -> p i f", i=ROWS)
             rows_a_store = 1 if b == BATCH - 1 else ROWS
             for i in range(ROWS):
@@ -183,9 +187,9 @@ def tile_agcrncell_pb_t_kernel(
         identity = keep.tile([P, P], F32)
         make_identity(nc, identity[:])
 
-        w_lin = keep.tile([P, KC // P * GATES], BF16)
+        w_lin = keep.tile([P, KC // P * GATES], BF16, align_bytes=DMA_ALIGN)
         nc.sync.dma_start(out=w_lin[:], in_=W_gate.rearrange("(p i) c -> p (i c)", p=P))
-        st_lin = keep.tile([P, BATCH * NODES // P * HID], BF16)
+        st_lin = keep.tile([P, BATCH * NODES // P * HID], BF16, align_bytes=DMA_ALIGN)
         nc.sync.dma_start(
             out=st_lin[:], in_=state.flatten_outer_dims().rearrange("(p r) h -> p (r h)", p=P)
         )
@@ -195,7 +199,7 @@ def tile_agcrncell_pb_t_kernel(
         ones = keep.tile([P, P], BF16)
         nc.vector.memset(ones[:], 1.0)
         load(0)
-        s_raw = keep.tile([P, ROWS * NODES], BF16)
+        s_raw = keep.tile([P, ROWS * NODES], BF16, align_bytes=DMA_ALIGN)
         nc.sync.dma_start(out=s_raw[:], in_=supports.rearrange("(p i) m -> p (i m)", i=ROWS))
         load(1)
         for b in range(2, PREFETCH):

@@ -21,6 +21,7 @@ GATE_PASSES = KC // K_PASS
 ROWS = NODES // P
 
 DMA_ALIGN = 256
+STREAM_ALIGN = 4096
 
 PREFETCH = 3
 
@@ -56,10 +57,10 @@ def tile_agcrncell_pb_t_kernel(
         zr_sb, cand_f32, cand_grouped = {}, {}, {}
 
         def load(b):
-            xg_sb[b] = inputs.tile([P, ROWS * KC], BF16, align_bytes=DMA_ALIGN, name="xg_sb")
+            xg_sb[b] = inputs.tile([P, ROWS * KC], BF16, align_bytes=STREAM_ALIGN, name="xg_sb")
             nc.sync.dma_start(out=xg_sb[b][:], in_=xg[b].rearrange("(p j) k -> p (j k)", j=ROWS))
             x_sb[b] = inputs.tile(
-                [P, ROWS, DIN], BF16, align_bytes=DMA_ALIGN, name="x_sb", bufs=PREFETCH + 2
+                [P, ROWS, DIN], BF16, align_bytes=STREAM_ALIGN, name="x_sb", bufs=PREFETCH + 2
             )
             nc.sync.dma_start(out=x_sb[b][:], in_=x[b].rearrange("(p j) f -> p j f", j=ROWS))
 
@@ -123,7 +124,7 @@ def tile_agcrncell_pb_t_kernel(
             )
 
         def x_part(b):
-            cand_f32[b] = results.tile([P, ROWS, FEAT], F32, align_bytes=DMA_ALIGN, name="cand_f32")
+            cand_f32[b] = results.tile([P, ROWS, FEAT], F32, align_bytes=STREAM_ALIGN, name="cand_f32")
             nc.vector.tensor_copy(out=cand_f32[b][:, :, :DIN], in_=x_sb[b][:])
             cand_grouped[b] = work.tile(
                 [P, FEAT, PACK], BF16, align_bytes=64, name="cand_grouped"
@@ -165,7 +166,7 @@ def tile_agcrncell_pb_t_kernel(
             return cand_codes, cand_scales
 
         def hop(b, cand_codes, cand_scales):
-            c1_sb = results.tile([P, ROWS, FEAT], F32, align_bytes=DMA_ALIGN)
+            c1_sb = results.tile([P, ROWS, FEAT], F32, align_bytes=STREAM_ALIGN)
             c1_rows = c1_out[b].rearrange("(p i) f -> p i f", i=ROWS)
             rows_a_store = 1 if b == BATCH - 1 else ROWS
             for i in range(ROWS):
@@ -179,7 +180,10 @@ def tile_agcrncell_pb_t_kernel(
                     start=True,
                     stop=True,
                 )
-                nc.scalar.copy(out=c1_sb[:, i, :], in_=c1_ps[:])
+                if b == BATCH - 1 and i % 2 == 1:
+                    nc.vector.tensor_copy(out=c1_sb[:, i, :], in_=c1_ps[:])
+                else:
+                    nc.scalar.copy(out=c1_sb[:, i, :], in_=c1_ps[:])
                 if (i + 1) % rows_a_store == 0:
                     ready = slice(i + 1 - rows_a_store, i + 1)
                     nc.sync.dma_start(out=c1_rows[:, ready, :], in_=c1_sb[:, ready, :])
@@ -306,7 +310,9 @@ def tile_agcrncell_pb_t_kernel(
             if 0 <= second < BATCH:
                 gate_matmul(second)
                 x_part(second)
+            if second == BATCH - 1:
+                gate_sigmoid(second)
             if third >= 0:
                 hop(third, cand_codes, cand_scales)
-            if 0 <= second < BATCH:
+            if 0 <= second < BATCH - 1:
                 gate_sigmoid(second)

from contextlib import ExitStack

import concourse.mybir as mybir
from concourse.masks import make_identity

BF16 = mybir.dt.bfloat16
F32 = mybir.dt.float32
U32 = mybir.dt.uint32
U8 = mybir.dt.uint8
FP8X4 = mybir.dt.float8_e4m3fn_x4

P = 128
PACK = 4
K_PASS = P * PACK

BATCH, NODES, DIN, HID = 8, 512, 448, 64
FEAT = DIN + HID
KC = 3 * FEAT
GATES = 2 * HID
GATE_PASSES = KC // K_PASS
ROWS = NODES // P

DMA_ALIGN = 256
STREAM_ALIGN = 4096

PREFETCH = 3

FLOPS = 2 * BATCH * NODES * KC * GATES + 2 * BATCH * NODES * NODES * FEAT


def words_onto_partitions(nc, banks, identity, blocks, grouped_words):
    bank = banks.tile([P, 2, 2, P], F32)
    for s in range(2):
        for u in range(2):
            nc.tensor.transpose(out=bank[:, s, u, :], in_=blocks[s][u], identity=identity)
    nc.scalar.copy(out=grouped_words, in_=bank[:].rearrange("q s u r -> q s r u"))


def tile_agcrncell_pb_t_kernel(
    tc, xg, W_gate, b_gate, x, state, supports, out_0, out_1, out_2
):
    nc = tc.nc
    r_out, cand_out, c1_out = out_0, out_1, out_2

    with ExitStack() as ctx:
        keep = ctx.enter_context(tc.tile_pool(name="keep", bufs=1))
        inputs = ctx.enter_context(tc.tile_pool(name="inputs", bufs=PREFETCH + 1))
        work = ctx.enter_context(tc.tile_pool(name="work", bufs=2))
        results = ctx.enter_context(tc.tile_pool(name="results", bufs=4))
        banks = ctx.enter_context(tc.psum_pool(name="banks", bufs=4))
        gate_banks = ctx.enter_context(tc.psum_pool(name="gate_banks", bufs=1))
        hop_banks = ctx.enter_context(tc.psum_pool(name="hop_banks", bufs=3))
        ctx.enter_context(tc.manual_schedule())

        xg_sb, x_sb = {}, {}
        xg_codes, xg_scales = {}, {}
        zr_sb, cand_f32, cand_grouped = {}, {}, {}

        def load(b):
            xg_sb[b] = inputs.tile([P, ROWS * KC], BF16, align_bytes=STREAM_ALIGN, name="xg_sb")
            nc.sync.dma_start(out=xg_sb[b][:], in_=xg[b].rearrange("(p j) k -> p (j k)", j=ROWS))
            x_sb[b] = inputs.tile(
                [P, ROWS, DIN], BF16, align_bytes=STREAM_ALIGN, name="x_sb", bufs=PREFETCH + 2
            )
            nc.sync.dma_start(out=x_sb[b][:], in_=x[b].rearrange("(p j) f -> p j f", j=ROWS))

        def turn_xg(b):
            xg_codes[b] = work.tile(
                [P, GATE_PASSES, ROWS * P], U32, align_bytes=64, name="xg_codes"
            )
            xg_scales[b] = work.tile(
                [P, GATE_PASSES, ROWS * P], U8, align_bytes=64, name="xg_scales"
            )
            xg_grouped = [
                work.tile(
                    [P, ROWS * P * PACK], BF16, align_bytes=64, name="xg_grouped", bufs=GATE_PASSES
                )
                for g in range(GATE_PASSES)
            ]
            xg_words = xg_sb[b][:].bitcast(F32).rearrange(
                "p (j g u q) -> p j g u q", j=ROWS, g=GATE_PASSES, u=2
            )
            for j in range(0, ROWS, 2):
                for g in range(GATE_PASSES):
                    xg_grouped_words = xg_grouped[g][:].bitcast(F32).rearrange(
                        "q (j r u) -> q j r u", j=ROWS, u=2
                    )
                    words_onto_partitions(
                        nc,
                        banks,
                        identity[:],
                        [[xg_words[:, j + s, g, u, :] for u in range(2)] for s in range(2)],
                        xg_grouped_words[:, j : j + 2, :, :],
                    )
            for g in range(GATE_PASSES):
                nc.vector.quantize_mx(
                    out=xg_codes[b][:, g, :].bitcast(FP8X4),
                    scales=xg_scales[b][:, g, :],
                    in_=xg_grouped[g][:],
                )

        def gate_matmul(b):
            zr_ps = gate_banks.tile([P, ROWS, GATES], F32)
            for j in range(ROWS):
                rows = slice(j * P, (j + 1) * P)
                for g in range(GATE_PASSES):
                    nc.tensor.matmul_mx(
                        out=zr_ps[:, j, :],
                        lhsT=xg_codes[b][:, g, rows].bitcast(FP8X4),
                        lhsT_scale=xg_scales[b][:, g, rows],
                        rhs=w_codes[:, g, :].bitcast(FP8X4),
                        rhs_scale=w_scales[:, g, :],
                        start=(g == 0),
                        stop=(g == GATE_PASSES - 1),
                    )
            zr_sb[b] = results.tile([P, 2, ROWS, HID], F32, align_bytes=DMA_ALIGN, name="zr_sb")
            nc.vector.tensor_tensor(
                out=zr_sb[b][:].rearrange("p h j c -> p j h c"),
                in0=zr_ps[:].rearrange("p j (h c) -> p j h c", h=2),
                in1=bias[:].rearrange("p (o h c) -> p o h c", o=1, h=2).to_broadcast(
                    [P, ROWS, 2, HID]
                ),
                op=mybir.AluOpType.add,
            )

        def x_part(b):
            cand_f32[b] = results.tile([P, ROWS, FEAT], F32, align_bytes=STREAM_ALIGN, name="cand_f32")
            nc.vector.tensor_copy(out=cand_f32[b][:, :, :DIN], in_=x_sb[b][:])
            cand_grouped[b] = work.tile(
                [P, FEAT, PACK], BF16, align_bytes=64, name="cand_grouped"
            )
            nc.vector.tensor_copy(
                out=cand_grouped[b][:, :DIN, :].rearrange("q (c i) t -> q c t i", i=4),
                in_=x_sb[b][:].rearrange("q t (c i) -> q c t i", i=4),
            )

        def gate_sigmoid(b):
            nc.scalar.activation(
                out=zr_sb[b][:], in_=zr_sb[b][:], func=mybir.ActivationFunctionType.Sigmoid
            )
            nc.sync.dma_start(
                out=r_out[b].rearrange("(p j) h -> p j h", j=ROWS), in_=zr_sb[b][:, 1, :, :]
            )

        def finish_cand(b):
            nc.vector.tensor_tensor(
                out=cand_f32[b][:, :, DIN:],
                in0=zr_sb[b][:, 0, :, :],
                in1=state_sb[:, b, :, :],
                op=mybir.AluOpType.mult,
            )
            nc.sync.dma_start(
                out=cand_out[b].rearrange("(p j) f -> p j f", j=ROWS), in_=cand_f32[b][:]
            )
            nc.vector.tensor_copy(
                out=cand_grouped[b][:, DIN:, :],
                in_=cand_f32[b][:, :, DIN:].rearrange("q t f -> q f t"),
            )
            cand_codes = work.tile([P, FEAT], U32, align_bytes=64)
            cand_scales = work.tile([P, FEAT], U8, align_bytes=64)
            nc.vector.quantize_mx(
                out=cand_codes[:].bitcast(FP8X4),
                scales=cand_scales[:],
                in_=cand_grouped[b][:].rearrange("q f t -> q (f t)"),
            )
            return cand_codes, cand_scales

        def hop(b, cand_codes, cand_scales):
            c1_sb = results.tile([P, ROWS, FEAT], F32, align_bytes=STREAM_ALIGN)
            c1_rows = c1_out[b].rearrange("(p i) f -> p i f", i=ROWS)
            rows_a_store = 1 if b == BATCH - 1 else ROWS
            for i in range(ROWS):
                c1_ps = hop_banks.tile([P, FEAT], F32)
                nc.tensor.matmul_mx(
                    out=c1_ps[:],
                    lhsT=s_codes[:, i, :].bitcast(FP8X4),
                    lhsT_scale=s_scales[:, i, :],
                    rhs=cand_codes[:].bitcast(FP8X4),
                    rhs_scale=cand_scales[:],
                    start=True,
                    stop=True,
                )
                if b == BATCH - 1 and i % 2 == 1:
                    nc.vector.tensor_copy(out=c1_sb[:, i, :], in_=c1_ps[:])
                else:
                    nc.scalar.copy(out=c1_sb[:, i, :], in_=c1_ps[:])
                if (i + 1) % rows_a_store == 0:
                    ready = slice(i + 1 - rows_a_store, i + 1)
                    nc.sync.dma_start(out=c1_rows[:, ready, :], in_=c1_sb[:, ready, :])

        identity = keep.tile([P, P], F32)
        make_identity(nc, identity[:])

        w_lin = keep.tile([P, KC // P * GATES], BF16, align_bytes=DMA_ALIGN)
        nc.sync.dma_start(out=w_lin[:], in_=W_gate.rearrange("(p i) c -> p (i c)", p=P))
        st_lin = keep.tile([P, BATCH * NODES // P * HID], BF16, align_bytes=DMA_ALIGN)
        nc.sync.dma_start(
            out=st_lin[:], in_=state.flatten_outer_dims().rearrange("(p r) h -> p (r h)", p=P)
        )
        bias_rows = keep.tile([P, GATES], BF16)
        nc.vector.memset(bias_rows[:], 0.0)
        nc.sync.dma_start(out=bias_rows[0:1, :], in_=b_gate.rearrange("(o c) -> o c", o=1))
        ones = keep.tile([P, P], BF16)
        nc.vector.memset(ones[:], 1.0)
        load(0)
        s_raw = keep.tile([P, ROWS * NODES], BF16, align_bytes=DMA_ALIGN)
        nc.sync.dma_start(out=s_raw[:], in_=supports.rearrange("(p i) m -> p (i m)", i=ROWS))
        load(1)
        for b in range(2, PREFETCH):
            load(b)

        w_codes = keep.tile([P, GATE_PASSES, GATES], U32, align_bytes=64)
        w_scales = keep.tile([P, GATE_PASSES, GATES], U8, align_bytes=64)
        s_codes = keep.tile([P, ROWS, P], U32, align_bytes=64)
        s_scales = keep.tile([P, ROWS, P], U8, align_bytes=64)

        bias = keep.tile([P, GATES], F32)

        def spread_bias():
            bias_ps = banks.tile([P, GATES], F32, tag="bank")
            nc.tensor.matmul(out=bias_ps[:], lhsT=ones[:], rhs=bias_rows[:], start=True, stop=True)
            nc.scalar.copy(out=bias[:], in_=bias_ps[:])

        def turned(words, count):
            filled = []
            for first in range(0, count, 4):
                bank = banks.tile([P, 4, P], F32, tag="bank", name="turned_bank")
                for n in range(first, min(first + 4, count)):
                    nc.tensor.transpose(
                        out=bank[:, n - first, :], in_=words[:, n * P : (n + 1) * P], identity=identity[:]
                    )
                filled.append(bank[:, : min(4, count - first), :])
            return filled

        w_raw = keep.tile([P, GATE_PASSES, PACK, GATES], BF16)

        def sort_w_gate():
            pairs_of_rows = KC // P // 2
            w_half = keep.tile([P, P, pairs_of_rows], F32)
            low, high = turned(w_lin[:].bitcast(F32), pairs_of_rows)
            nc.scalar.copy(out=w_half[:, :, :4], in_=low.rearrange("q m p -> q p m"))
            nc.vector.tensor_copy(out=w_half[:, :, 4:], in_=high.rearrange("q m p -> q p m"))
            low, high = turned(w_half[:].rearrange("q p m -> q (p m)"), pairs_of_rows)
            w_raw_words = w_raw[:].rearrange("q g t c -> q (g t c)").bitcast(F32).rearrange(
                "q (s w) -> q s w", w=P
            )
            nc.scalar.copy(out=w_raw_words[:, :4, :], in_=low)
            nc.vector.tensor_copy(out=w_raw_words[:, 4:, :], in_=high)

        state_sb = keep.tile([P, BATCH, ROWS, HID], BF16)

        def sort_state():
            blocks = BATCH * NODES // P // ROWS
            st_half = keep.tile([P, P, blocks], F32)
            low, high = turned(st_lin[:].bitcast(F32), blocks)
            nc.scalar.copy(out=st_half[:, :, :4], in_=low.rearrange("q v p -> q p v"))
            nc.vector.tensor_copy(out=st_half[:, :, 4:], in_=high.rearrange("q v p -> q p v"))
            low, high = turned(st_half[:].rearrange("q p v -> q (p v)"), BATCH)
            state_words = state_sb[:].rearrange("p b j h -> p (b j h)").bitcast(F32).rearrange(
                "p (b w) -> p b w", b=BATCH
            )
            nc.scalar.copy(out=state_words[:, :4, :], in_=low)
            nc.vector.tensor_copy(out=state_words[:, 4:, :], in_=high)

        def quantise_w_gate():
            w_grouped = keep.tile([P, GATE_PASSES, GATES, PACK], BF16, align_bytes=64)
            nc.vector.tensor_copy(out=w_grouped[:], in_=w_raw[:].rearrange("q g t c -> q g c t"))
            for g in range(GATE_PASSES):
                nc.vector.quantize_mx(
                    out=w_codes[:, g, :].bitcast(FP8X4),
                    scales=w_scales[:, g, :],
                    in_=w_grouped[:, g, :, :].rearrange("q c t -> q (c t)"),
                )

        def turn_supports():
            s_words = s_raw[:].bitcast(F32).rearrange("p (i q u) -> p i u q", i=ROWS, u=2)
            s_grouped = keep.tile([P, ROWS * P * PACK], BF16, align_bytes=64)
            s_grouped_words = s_grouped[:].bitcast(F32).rearrange(
                "q (i r u) -> q i r u", i=ROWS, u=2
            )
            for i in range(0, ROWS, 2):
                words_onto_partitions(
                    nc,
                    banks,
                    identity[:],
                    [[s_words[:, i + s, u, :] for u in range(2)] for s in range(2)],
                    s_grouped_words[:, i : i + 2, :, :],
                )
            nc.vector.quantize_mx(
                out=s_codes[:].rearrange("q i r -> q (i r)").bitcast(FP8X4),
                scales=s_scales[:].rearrange("q i r -> q (i r)"),
                in_=s_grouped[:],
            )

        sort_w_gate()
        sort_state()
        quantise_w_gate()
        spread_bias()

        for step in range(BATCH + 2):
            first, second, third = step, step - 1, step - 2
            if first + PREFETCH < BATCH:
                load(first + PREFETCH)
            if third >= 0:
                cand_codes, cand_scales = finish_cand(third)
            if first < BATCH:
                turn_xg(first)
            if step == 0:
                turn_supports()
            if 0 <= second < BATCH:
                gate_matmul(second)
                x_part(second)
            if second == BATCH - 1:
                gate_sigmoid(second)
            if third >= 0:
                hop(third, cand_codes, cand_scales)
            if 0 <= second < BATCH - 1:
                gate_sigmoid(second)
